import numpy as np
import ml_dtypes


def mxq(x, axis, fmt="e4m3"):
    dtype, down = {"e4m3": (ml_dtypes.float8_e4m3fn, 7), "e5m2": (ml_dtypes.float8_e5m2, 14)}[fmt]
    v = np.moveaxis(np.asarray(x, np.float32).astype(ml_dtypes.bfloat16).astype(np.float64), axis, -1)
    blocks = v.reshape(v.shape[:-1] + (-1, 32))
    amax = np.abs(blocks).max(-1, keepdims=True)
    byte = np.maximum(np.where(amax > 0, np.frexp(amax)[1] - 1 + 127, 0) - down, 1)
    scale = np.exp2(byte - 127.0)
    codes = (blocks / scale).astype(np.float32).astype(dtype).astype(np.float64)
    return np.moveaxis((codes * scale).reshape(v.shape), -1, axis)


WIDE = False


def mx_kscale(k):
    if not WIDE:
        return np.ones(k)
    levels = np.array([10, -10, 5, -5, 0])
    a = np.random.permutation(np.resize(levels, k // 512 * 4)).reshape(k // 512, 4)
    idx = np.arange(k)
    return np.exp2(a[idx // 512, idx % 128 // 32])


BF16 = ml_dtypes.bfloat16


def bf(x):
    return np.asarray(x, np.float32).astype(BF16)


def f64(x):
    return np.asarray(x).astype(np.float64)


E2M1 = np.array([0.0, 0.5, 1.0, 1.5, 2.0, 3.0, 4.0, 6.0, -0.0, -0.5, -1.0, -1.5, -2.0, -3.0, -4.0, -6.0])


def pack_weight(w, fmt):
    k, n = w.shape
    w = f64(bf(w)).reshape(k // 32, 32, n)
    amax = np.abs(w).max(1)
    if fmt == "e4m3":
        byte = np.frexp(amax)[1] - 1 + 127 - 7
    else:
        mant, ex = np.frexp(amax / 6.0)
        byte = np.where(mant > 0.5, ex, ex - 1) + 127
    byte = np.clip(np.where(amax > 0, byte, 1), 1, 254)
    scaled = (w * np.exp2(127.0 - byte)[:, None, :]).reshape(k, n).astype(np.float32)
    by_word = np.ascontiguousarray(scaled.reshape(k // 512, 128, 4, n).transpose(0, 1, 3, 2))
    if fmt == "e4m3":
        words = by_word.astype(ml_dtypes.float8_e4m3fn).view(np.uint8)
    else:
        c = by_word.astype(ml_dtypes.float4_e2m1fn).view(np.uint8) & 0xF
        words = c[..., 0::2] | (c[..., 1::2] << 4)
    return np.ascontiguousarray(words), np.ascontiguousarray(byte.astype(np.uint8).reshape(k // 512, 16, n))


def unpack_weight(words, scales, fmt):
    g, p, n, _ = words.shape
    if fmt == "e4m3":
        vals = np.ascontiguousarray(words).view(ml_dtypes.float8_e4m3fn).astype(np.float64)
    else:
        nib = np.empty((g, p, n, 4), np.uint8)
        nib[..., 0::2] = words & 0xF
        nib[..., 1::2] = words >> 4
        vals = E2M1[nib]
    vals = vals * np.repeat(np.exp2(scales.astype(np.float64) - 127.0), 8, axis=1)[..., None]
    return vals.transpose(0, 1, 3, 2).reshape(g * 512, n)

def pack4(w):
    words, scales = pack_weight(w, "e2m1")
    return words.reshape(words.shape[0], 128, -1), scales


def unpack4(words, scales):
    return unpack_weight(words.reshape(words.shape[0], 128, -1, 2), scales, "e2m1")


T, B, D, U, V, E = 4, 256, 512, 512, 512, 8
G = 2 * E
GS = (T + 1) * E
N = U * E


def softmax(v):
    e = np.exp(v - v.max(-1, keepdims=True))
    return e / e.sum(-1, keepdims=True)


def setup_inputs():
    rn = np.random.standard_normal
    s = mx_kscale(D)
    x = bf(rn((B, D)) * s)
    ews0_words, ews0_scales = pack4((rn((D, U, E)) / np.sqrt(D) / s[:, None, None]).reshape(D, N))
    ebs0 = bf(rn((U, E)) * 0.5)
    stack = (rn((T, D, U, E)) / np.sqrt(D) / s[None, :, None, None]).reshape(T, D, N)
    ew0_words, ew0_scales = pack4(stack.reshape(-1, N))
    return {
        "x": x,
        "ews0_words": ews0_words,
        "ews0_scales": ews0_scales,
        "ebs0": ebs0,
        "ew0_words": ew0_words,
        "ew0_scales": ew0_scales,
        "eb0": bf(rn((T, U, E)) * 0.5),
        "gate_pre0": bf(rn((T, B, G))),
        "gb0": bf(rn((T, G)) * 0.5),
        "sgate_pre": bf(rn((B, GS))),
        "gbs": bf(rn((GS,)) * 0.5),
    }


def reference(x, ews0_words, ews0_scales, ebs0, ew0_words, ew0_scales, eb0, gate_pre0, gb0, sgate_pre, gbs):
    xq = mxq(f64(x), 1, "e4m3")
    es = np.maximum((xq @ unpack4(ews0_words, ews0_scales)).reshape(B, U, E) + f64(ebs0), 0.0)
    et = np.maximum((xq @ unpack4(ew0_words, ew0_scales).reshape(T, D, N)).reshape(T, B, U, E) + f64(eb0)[:, None], 0.0)
    g = softmax(f64(gate_pre0) + f64(gb0)[:, None])
    comb = np.concatenate([et, np.broadcast_to(es, et.shape)], axis=-1)
    task_out = (comb * g[:, :, None, :]).sum(-1)
    gs = softmax(f64(sgate_pre) + f64(gbs))
    all_exp = np.concatenate([np.moveaxis(et, 0, 2).reshape(B, U, T * E), es], axis=-1)
    share_out = (all_exp * gs[:, None, :]).sum(-1)
    return task_out, share_out

@@ -1,0 +1,201 @@
+from contextlib import ExitStack
+
+import concourse.mybir as mybir
+from concourse.masks import make_identity
+
+F32 = mybir.dt.float32
+BF16 = mybir.dt.bfloat16
+I32 = mybir.dt.int32
+U8 = mybir.dt.uint8
+U32 = mybir.dt.uint32
+FP8X4 = mybir.dt.float8_e4m3fn_x4
+FP4X4 = mybir.dt.float4_e2m1fn_x4
+ALU = mybir.AluOpType
+ACT = mybir.ActivationFunctionType
+AXIS = mybir.AxisListType
+
+P = 128
+TASKS = 4
+BATCH = 256
+ROW_TILES = BATCH // P
+D = 512
+UNITS = 512
+EXPERTS = 8
+SOURCES = TASKS + 1
+SHARED = TASKS
+COLS = UNITS * EXPERTS
+PASS_COLS = 512
+PASS_UNITS = PASS_COLS // EXPERTS
+PASSES = COLS // PASS_COLS
+UNIT_BLOCKS = UNITS // P
+TASK_GATES = 2 * EXPERTS
+SHARE_GATES = SOURCES * EXPERTS
+
+FLOPS = 2 * BATCH * D * COLS * SOURCES
+
+
+def tile_plelayer_pa_e_kernel(
+    tc, x, ews0_words, ews0_scales, ebs0, ew0_words, ew0_scales, eb0, gate_pre0, gb0, sgate_pre, gbs, out_0, out_1
+):
+    nc = tc.nc
+    with ExitStack() as ctx:
+        keep = ctx.enter_context(tc.tile_pool(name="keep", bufs=1))
+        pre_pool = ctx.enter_context(tc.tile_pool(name="pre", bufs=2))
+        term_pool = ctx.enter_context(tc.tile_pool(name="term", bufs=8))
+        out_pool = ctx.enter_context(tc.tile_pool(name="outp", bufs=2))
+        psum_acc = ctx.enter_context(tc.psum_pool(name="psum_acc", bufs=3))
+        psum_sum = ctx.enter_context(tc.psum_pool(name="psum_sum", bufs=3))
+        psum_turn = ctx.enter_context(tc.psum_pool(name="psum_turn", bufs=2))
+
+        x_sb = keep.tile([P, ROW_TILES, D], BF16, name="x_sb")
+        nc.sync.dma_start(out=x_sb[:], in_=x.rearrange("(h p) d -> p h d", p=P))
+
+        words = keep.tile([P, SOURCES, 2 * COLS], U8, name="words", align_bytes=64)
+        planes = keep.tile([P, SOURCES, COLS], U8, name="planes", align_bytes=64)
+        bias_all = keep.tile([P, SOURCES, COLS], BF16, name="bias_all")
+        for s in (SHARED, 0, 1, 2, 3):
+            src_words = ews0_words[0] if s == SHARED else ew0_words[s]
+            src_scales = ews0_scales[0] if s == SHARED else ew0_scales[s]
+            src_bias = ebs0 if s == SHARED else eb0[s]
+            nc.vector.memset(planes[:, s, :].bitcast(I32), 0)
+            for quad in range(4):
+                nc.sync.dma_start(
+                    out=planes[32 * quad : 32 * quad + 4, s, :].bitcast(I32),
+                    in_=src_scales[4 * quad : 4 * quad + 4, :].bitcast(I32),
+                )
+            nc.sync.dma_start(out=words[:, s, :].bitcast(I32), in_=src_words.bitcast(I32))
+            nc.gpsimd.dma_start(
+                out=bias_all[:, s, :], in_=src_bias.rearrange("u e -> (u e)").partition_broadcast(P)
+            )
+
+        pre_task = keep.tile([P, ROW_TILES, TASKS * TASK_GATES], BF16, name="pre_task")
+        for h in range(ROW_TILES):
+            nc.scalar.dma_start(
+                out=pre_task[:, h, :].rearrange("p (t g) -> p t g", g=TASK_GATES),
+                in_=gate_pre0[:, h * P : (h + 1) * P, :].rearrange("t p g -> p t g"),
+            )
+        pre_share = keep.tile([P, ROW_TILES, SHARE_GATES], BF16, name="pre_share")
+        nc.scalar.dma_start(out=pre_share[:], in_=sgate_pre.rearrange("(h p) g -> p h g", p=P))
+        gb_task = keep.tile([P, TASKS * TASK_GATES], BF16, name="gb_task")
+        nc.scalar.dma_start(out=gb_task[:], in_=gb0.rearrange("t g -> (t g)").partition_broadcast(P))
+        gb_share = keep.tile([P, SHARE_GATES], BF16, name="gb_share")
+        nc.scalar.dma_start(out=gb_share[:], in_=gbs.partition_broadcast(P))
+
+        ident = keep.tile([P, P], F32, name="ident")
+        make_identity(nc, ident[:])
+
+        x_turn = psum_turn.tile([P, ROW_TILES, 2, P], F32, name="x_turn", tag="turn")
+        for h in range(ROW_TILES):
+            x_words = x_sb[:, h, :].bitcast(F32)
+            for v in range(2):
+                nc.tensor.transpose(x_turn[:, h, v, :], x_words[:, v : D // 2 : 2], ident[:])
+        x_grouped = keep.tile([P, BATCH * 4], BF16, name="x_grouped", align_bytes=64)
+        nc.vector.tensor_copy(
+            out=x_grouped[:].bitcast(F32).rearrange("p (h b v) -> p h b v", h=ROW_TILES, v=2),
+            in_=x_turn[:].rearrange("p h v b -> p h b v"),
+        )
+        x_codes = keep.tile([P, BATCH], U32, name="x_codes", align_bytes=64)
+        x_scales = keep.tile([P, BATCH], U8, name="x_scales", align_bytes=64)
+        nc.vector.quantize_mx(out=x_codes[:].bitcast(FP8X4), scales=x_scales[:], in_=x_grouped[:])
+
+        def softmax_groups(pre, bias, width, name):
+            entries = pre.shape[2]
+            groups = ROW_TILES * entries // width
+            gate = keep.tile([P, ROW_TILES, entries], F32, name=name)
+            top = keep.tile([P, groups], F32, name=name + "_top")
+            total = keep.tile([P, groups], F32, name=name + "_total")
+            grouped = gate[:].rearrange("p h (n g) -> p (h n) g", g=width)
+            nc.vector.tensor_tensor(
+                out=gate[:], in0=pre, in1=bias.unsqueeze(1).to_broadcast([P, ROW_TILES, entries]), op=ALU.add
+            )
+            nc.vector.tensor_reduce(out=top[:], in_=grouped, axis=AXIS.X, op=ALU.max)
+            nc.vector.tensor_tensor(
+                out=grouped, in0=grouped, in1=top[:].unsqueeze(2).to_broadcast([P, groups, width]), op=ALU.subtract
+            )
+            nc.scalar.activation(out=gate[:], in_=gate[:], func=ACT.Exp)
+            nc.vector.tensor_reduce(out=total[:], in_=grouped, axis=AXIS.X, op=ALU.add)
+            nc.vector.reciprocal(out=total[:], in_=total[:])
+            nc.vector.tensor_tensor(
+                out=grouped, in0=grouped, in1=total[:].unsqueeze(2).to_broadcast([P, groups, width]), op=ALU.mult
+            )
+            return gate
+
+        gate_task = softmax_groups(pre_task[:], gb_task[:], TASK_GATES, "gate_task")
+        gate_share = softmax_groups(pre_share[:], gb_share[:], SHARE_GATES, "gate_share")
+
+        def expert_preactivations(s, h, tag):
+            pre = pre_pool.tile([P, EXPERTS, UNITS], F32, name="pre_" + tag, tag=tag)
+            for c in range(PASSES):
+                acc = psum_acc.tile([P, PASS_COLS], F32, name="acc")
+                nc.tensor.matmul_mx(
+                    out=acc[:],
+                    lhsT=x_codes[:, h * P : (h + 1) * P].bitcast(FP8X4),
+                    lhsT_scale=x_scales[:, h * P : (h + 1) * P],
+                    rhs=words[:, s, 2 * c * PASS_COLS : 2 * (c + 1) * PASS_COLS].bitcast(FP4X4),
+                    rhs_scale=planes[:, s, c * PASS_COLS : (c + 1) * PASS_COLS],
+                    start=True,
+                    stop=True,
+                )
+                nc.vector.tensor_tensor(
+                    out=pre[:, :, c * PASS_UNITS : (c + 1) * PASS_UNITS],
+                    in0=acc[:].rearrange("p (u e) -> p e u", e=EXPERTS),
+                    in1=bias_all[:, s, c * PASS_COLS : (c + 1) * PASS_COLS].rearrange("p (u e) -> p e u", e=EXPERTS),
+                    op=ALU.add,
+                )
+            return pre
+
+        def add_term(total, pre, e, gate_column, first, last):
+            term = term_pool.tile([P, UNITS], F32, name="term")
+            if e % 2 == 0:
+                nc.scalar.activation(out=term[:], in_=pre[:, e, :], func=ACT.Relu, scale=gate_column)
+            else:
+                nc.vector.tensor_scalar(
+                    out=term[:], in0=pre[:, e, :], scalar1=gate_column, scalar2=0.0, op0=ALU.mult, op1=ALU.max
+                )
+            for k in range(UNIT_BLOCKS):
+                nc.tensor.matmul(
+                    out=total[:, k, :],
+                    lhsT=term[:, k * P : (k + 1) * P],
+                    rhs=ident[:],
+                    is_transpose=True,
+                    start=(first and k == 0),
+                    stop=(last and k == UNIT_BLOCKS - 1),
+                )
+
+        def store(total, rows):
+            turned_in = out_pool.tile([P, UNIT_BLOCKS, P], F32, name="turned_in")
+            nc.scalar.copy(out=turned_in[:], in_=total[:])
+            turned = psum_turn.tile([P, UNIT_BLOCKS, P], F32, name="turned", tag="turn")
+            for k in range(UNIT_BLOCKS):
+                nc.tensor.transpose(turned[:, k, :], turned_in[:, k, :], ident[:])
+            result = out_pool.tile([P, UNITS], F32, name="result")
+            nc.vector.tensor_copy(out=result[:], in_=turned[:].rearrange("p k u -> p (k u)"))
+            nc.sync.dma_start(out=rows, in_=result[:])
+
+        for h in range(ROW_TILES):
+            rows = slice(h * P, (h + 1) * P)
+            share_total = psum_sum.tile([P, UNIT_BLOCKS, P], F32, name="share_total", tag="total")
+            shared_pre = expert_preactivations(SHARED, h, "shared")
+            for e in range(EXPERTS):
+                j = SHARED * EXPERTS + e
+                add_term(share_total, shared_pre, e, gate_share[:, h, j : j + 1], e == 0, False)
+            for t in range(TASKS):
+                own_pre = expert_preactivations(t, h, "own")
+                task_total = psum_sum.tile([P, UNIT_BLOCKS, P], F32, name="task_total", tag="total")
+                g = t * TASK_GATES
+                for e in range(EXPERTS):
+                    j = t * EXPERTS + e
+                    add_term(task_total, own_pre, e, gate_task[:, h, g + e : g + e + 1], e == 0, False)
+                    add_term(
+                        task_total,
+                        shared_pre,
+                        e,
+                        gate_task[:, h, g + EXPERTS + e : g + EXPERTS + e + 1],
+                        False,
+                        e == EXPERTS - 1,
+                    )
+                    add_term(
+                        share_total, own_pre, e, gate_share[:, h, j : j + 1], False, t == TASKS - 1 and e == EXPERTS - 1
+                    )
+                store(task_total, out_0[t, rows, :])
+            store(share_total, out_1[rows, :])

@@ -31,6 +31,13 @@ UNIT_BLOCKS = UNITS // P
 TASK_GATES = 2 * EXPERTS
 SHARE_GATES = SOURCES * EXPERTS
 
+ROUNDS = ROW_TILES * SOURCES
+STEPS = ROUNDS * EXPERTS
+PASS_LEAD = 12
+GATE_LEAD = 2
+STORE_LAG = 2
+WORD_PIECES = 4
+
 FLOPS = 2 * BATCH * D * COLS * SOURCES
 
 
@@ -39,34 +46,20 @@ def tile_plelayer_pa_e_kernel(
 ):
     nc = tc.nc
     with ExitStack() as ctx:
+        ctx.enter_context(tc.manual_schedule())
         keep = ctx.enter_context(tc.tile_pool(name="keep", bufs=1))
-        pre_pool = ctx.enter_context(tc.tile_pool(name="pre", bufs=2))
-        term_pool = ctx.enter_context(tc.tile_pool(name="term", bufs=8))
+        pre_pool = ctx.enter_context(tc.tile_pool(name="pre", bufs=1))
+        term_pool = ctx.enter_context(tc.tile_pool(name="term", bufs=12))
         out_pool = ctx.enter_context(tc.tile_pool(name="outp", bufs=2))
         psum_acc = ctx.enter_context(tc.psum_pool(name="psum_acc", bufs=3))
         psum_sum = ctx.enter_context(tc.psum_pool(name="psum_sum", bufs=3))
         psum_turn = ctx.enter_context(tc.psum_pool(name="psum_turn", bufs=2))
 
+        ident = keep.tile([P, P], F32, name="ident")
+        make_identity(nc, ident[:])
+
         x_sb = keep.tile([P, ROW_TILES, D], BF16, name="x_sb")
         nc.sync.dma_start(out=x_sb[:], in_=x.rearrange("(h p) d -> p h d", p=P))
-
-        words = keep.tile([P, SOURCES, 2 * COLS], U8, name="words", align_bytes=64)
-        planes = keep.tile([P, SOURCES, COLS], U8, name="planes", align_bytes=64)
-        bias_all = keep.tile([P, SOURCES, COLS], BF16, name="bias_all")
-        for s in (SHARED, 0, 1, 2, 3):
-            src_words = ews0_words[0] if s == SHARED else ew0_words[s]
-            src_scales = ews0_scales[0] if s == SHARED else ew0_scales[s]
-            src_bias = ebs0 if s == SHARED else eb0[s]
-            nc.vector.memset(planes[:, s, :].bitcast(I32), 0)
-            for quad in range(4):
-                nc.sync.dma_start(
-                    out=planes[32 * quad : 32 * quad + 4, s, :].bitcast(I32),
-                    in_=src_scales[4 * quad : 4 * quad + 4, :].bitcast(I32),
-                )
-            nc.sync.dma_start(out=words[:, s, :].bitcast(I32), in_=src_words.bitcast(I32))
-            nc.gpsimd.dma_start(
-                out=bias_all[:, s, :], in_=src_bias.rearrange("u e -> (u e)").partition_broadcast(P)
-            )
 
         pre_task = keep.tile([P, ROW_TILES, TASKS * TASK_GATES], BF16, name="pre_task")
         for h in range(ROW_TILES):
@@ -81,8 +74,28 @@ def tile_plelayer_pa_e_kernel(
         gb_share = keep.tile([P, SHARE_GATES], BF16, name="gb_share")
         nc.scalar.dma_start(out=gb_share[:], in_=gbs.partition_broadcast(P))
 
-        ident = keep.tile([P, P], F32, name="ident")
-        make_identity(nc, ident[:])
+        words = keep.tile([P, SOURCES, 2 * COLS], U8, name="words", align_bytes=64)
+        planes = keep.tile([P, SOURCES, COLS], U8, name="planes", align_bytes=64)
+        bias_all = keep.tile([P, SOURCES, COLS], BF16, name="bias_all")
+        piece = 2 * COLS // WORD_PIECES
+        for s in (SHARED, 0, 1, 2, 3):
+            src_words = ews0_words[0] if s == SHARED else ew0_words[s]
+            src_scales = ews0_scales[0] if s == SHARED else ew0_scales[s]
+            src_bias = ebs0 if s == SHARED else eb0[s]
+            nc.vector.memset(planes[:, s, :].bitcast(I32), 0)
+            for quad in range(4):
+                nc.sync.dma_start(
+                    out=planes[32 * quad : 32 * quad + 4, s, :].bitcast(I32),
+                    in_=src_scales[4 * quad : 4 * quad + 4, :].bitcast(I32),
+                )
+            for w in range(WORD_PIECES):
+                nc.sync.dma_start(
+                    out=words[:, s, w * piece : (w + 1) * piece].bitcast(I32),
+                    in_=src_words[:, w * piece : (w + 1) * piece].bitcast(I32),
+                )
+            nc.gpsimd.dma_start(
+                out=bias_all[:, s, :], in_=src_bias.rearrange("u e -> (u e)").partition_broadcast(P)
+            )
 
         x_turn = psum_turn.tile([P, ROW_TILES, 2, P], F32, name="x_turn", tag="turn")
         for h in range(ROW_TILES):
@@ -123,35 +136,66 @@ def tile_plelayer_pa_e_kernel(
         gate_task = softmax_groups(pre_task[:], gb_task[:], TASK_GATES, "gate_task")
         gate_share = softmax_groups(pre_share[:], gb_share[:], SHARE_GATES, "gate_share")
 
-        def expert_preactivations(s, h, tag):
-            pre = pre_pool.tile([P, EXPERTS, UNITS], F32, name="pre_" + tag, tag=tag)
-            for c in range(PASSES):
-                acc = psum_acc.tile([P, PASS_COLS], F32, name="acc")
-                nc.tensor.matmul_mx(
-                    out=acc[:],
-                    lhsT=x_codes[:, h * P : (h + 1) * P].bitcast(FP8X4),
-                    lhsT_scale=x_scales[:, h * P : (h + 1) * P],
-                    rhs=words[:, s, 2 * c * PASS_COLS : 2 * (c + 1) * PASS_COLS].bitcast(FP4X4),
-                    rhs_scale=planes[:, s, c * PASS_COLS : (c + 1) * PASS_COLS],
-                    start=True,
-                    stop=True,
-                )
-                nc.vector.tensor_tensor(
-                    out=pre[:, :, c * PASS_UNITS : (c + 1) * PASS_UNITS],
-                    in0=acc[:].rearrange("p (u e) -> p e u", e=EXPERTS),
-                    in1=bias_all[:, s, c * PASS_COLS : (c + 1) * PASS_COLS].rearrange("p (u e) -> p e u", e=EXPERTS),
-                    op=ALU.add,
-                )
-            return pre
+        def row_tile_of(r):
+            return r // SOURCES
 
-        def add_term(total, pre, e, gate_column, first, last):
+        def source_of(r):
+            return SHARED if r % SOURCES == 0 else r % SOURCES - 1
+
+        pre_of = {}
+
+        def issue_pass(q):
+            r, c = divmod(q, PASSES)
+            h, s = row_tile_of(r), source_of(r)
+            if c == 0:
+                if s == SHARED:
+                    pre_of[r] = pre_pool.tile([P, EXPERTS, UNITS], F32, name="pre_shared", tag="shared", bufs=2)
+                else:
+                    pre_of[r] = pre_pool.tile([P, EXPERTS, UNITS], F32, name="pre_own", tag="own", bufs=3)
+            acc = psum_acc.tile([P, PASS_COLS], F32, name="acc")
+            nc.tensor.matmul_mx(
+                out=acc[:],
+                lhsT=x_codes[:, h * P : (h + 1) * P].bitcast(FP8X4),
+                lhsT_scale=x_scales[:, h * P : (h + 1) * P],
+                rhs=words[:, s, 2 * c * PASS_COLS : 2 * (c + 1) * PASS_COLS].bitcast(FP4X4),
+                rhs_scale=planes[:, s, c * PASS_COLS : (c + 1) * PASS_COLS],
+                start=True,
+                stop=True,
+            )
+            nc.vector.tensor_tensor(
+                out=pre_of[r][:, :, c * PASS_UNITS : (c + 1) * PASS_UNITS],
+                in0=acc[:].rearrange("p (u e) -> p e u", e=EXPERTS),
+                in1=bias_all[:, s, c * PASS_COLS : (c + 1) * PASS_COLS].rearrange("p (u e) -> p e u", e=EXPERTS),
+                op=ALU.add,
+            )
+
+        def gated(pre, e, gate_column, number):
             term = term_pool.tile([P, UNITS], F32, name="term")
-            if e % 2 == 0:
+            if number % 2 == 0:
                 nc.scalar.activation(out=term[:], in_=pre[:, e, :], func=ACT.Relu, scale=gate_column)
             else:
                 nc.vector.tensor_scalar(
                     out=term[:], in0=pre[:, e, :], scalar1=gate_column, scalar2=0.0, op0=ALU.mult, op1=ALU.max
                 )
+            return term
+
+        terms_of = {}
+
+        def gate_step(n):
+            r, e = divmod(n, EXPERTS)
+            h, s = row_tile_of(r), source_of(r)
+            j = s * EXPERTS + e
+            for_share = gated(pre_of[r], e, gate_share[:, h, j : j + 1], n)
+            if s == SHARED:
+                terms_of[n] = [for_share]
+            else:
+                g = s * TASK_GATES + e
+                shared_pre = pre_of[h * SOURCES]
+                own = gated(pre_of[r], e, gate_task[:, h, g : g + 1], n + 1)
+                shared = gated(shared_pre, e, gate_task[:, h, g + EXPERTS : g + EXPERTS + 1], n + 2)
+                terms_of[n] = [for_share, own, shared]
+
+        def add_term(total, term, first, last):
             for k in range(UNIT_BLOCKS):
                 nc.tensor.matmul(
                     out=total[:, k, :],
@@ -162,9 +206,27 @@ def tile_plelayer_pa_e_kernel(
                     stop=(last and k == UNIT_BLOCKS - 1),
                 )
 
-        def store(total, rows):
-            turned_in = out_pool.tile([P, UNIT_BLOCKS, P], F32, name="turned_in")
+        totals = {}
+
+        def sum_step(n):
+            r, e = divmod(n, EXPERTS)
+            s = source_of(r)
+            if e == 0 and s == SHARED:
+                totals["share"] = psum_sum.tile([P, UNIT_BLOCKS, P], F32, name="share_total", tag="total")
+            if e == 0 and s != SHARED:
+                totals["task"] = psum_sum.tile([P, UNIT_BLOCKS, P], F32, name="task_total", tag="total")
+            terms = terms_of[n]
+            add_term(totals["share"], terms[0], s == SHARED and e == 0, s == TASKS - 1 and e == EXPERTS - 1)
+            if s != SHARED:
+                add_term(totals["task"], terms[1], e == 0, False)
+                add_term(totals["task"], terms[2], False, e == EXPERTS - 1)
+
+        def leave_psum(total):
+            turned_in = out_pool.tile([P, UNIT_BLOCKS, P], F32, name="turned_in", bufs=3)
             nc.scalar.copy(out=turned_in[:], in_=total[:])
+            return turned_in
+
+        def turn_and_store(turned_in, rows):
             turned = psum_turn.tile([P, UNIT_BLOCKS, P], F32, name="turned", tag="turn")
             for k in range(UNIT_BLOCKS):
                 nc.tensor.transpose(turned[:, k, :], turned_in[:, k, :], ident[:])
@@ -172,30 +234,23 @@ def tile_plelayer_pa_e_kernel(
             nc.vector.tensor_copy(out=result[:], in_=turned[:].rearrange("p k u -> p (k u)"))
             nc.sync.dma_start(out=rows, in_=result[:])
 
-        for h in range(ROW_TILES):
-            rows = slice(h * P, (h + 1) * P)
-            share_total = psum_sum.tile([P, UNIT_BLOCKS, P], F32, name="share_total", tag="total")
-            shared_pre = expert_preactivations(SHARED, h, "shared")
-            for e in range(EXPERTS):
-                j = SHARED * EXPERTS + e
-                add_term(share_total, shared_pre, e, gate_share[:, h, j : j + 1], e == 0, False)
-            for t in range(TASKS):
-                own_pre = expert_preactivations(t, h, "own")
-                task_total = psum_sum.tile([P, UNIT_BLOCKS, P], F32, name="task_total", tag="total")
-                g = t * TASK_GATES
-                for e in range(EXPERTS):
-                    j = t * EXPERTS + e
-                    add_term(task_total, own_pre, e, gate_task[:, h, g + e : g + e + 1], e == 0, False)
-                    add_term(
-                        task_total,
-                        shared_pre,
-                        e,
-                        gate_task[:, h, g + EXPERTS + e : g + EXPERTS + e + 1],
-                        False,
-                        e == EXPERTS - 1,
-                    )
-                    add_term(
-                        share_total, own_pre, e, gate_share[:, h, j : j + 1], False, t == TASKS - 1 and e == EXPERTS - 1
-                    )
-                store(task_total, out_0[t, rows, :])
-            store(share_total, out_1[rows, :])
+        for q in range(PASS_LEAD):
+            issue_pass(q)
+        for n in range(GATE_LEAD):
+            gate_step(n)
+        leaving = {}
+        for n in range(STEPS + STORE_LAG):
+            if n + GATE_LEAD < STEPS:
+                gate_step(n + GATE_LEAD)
+            if n + PASS_LEAD < STEPS:
+                issue_pass(n + PASS_LEAD)
+            if n < STEPS:
+                sum_step(n)
+                r, e = divmod(n, EXPERTS)
+                h, s = row_tile_of(r), source_of(r)
+                if e == EXPERTS - 1 and s != SHARED:
+                    leaving[n + STORE_LAG] = [(leave_psum(totals["task"]), out_0[s, h * P : (h + 1) * P, :])]
+                if e == EXPERTS - 1 and s == TASKS - 1:
+                    leaving[n + STORE_LAG].append((leave_psum(totals["share"]), out_1[h * P : (h + 1) * P, :]))
+            for turned_in, rows in leaving.get(n, []):
+                turn_and_store(turned_in, rows)

@@ -195,16 +195,15 @@ def tile_plelayer_pa_e_kernel(
                 shared = gated(shared_pre, e, gate_task[:, h, g + EXPERTS : g + EXPERTS + 1], n + 2)
                 terms_of[n] = [for_share, own, shared]
 
-        def add_term(total, term, first, last):
-            for k in range(UNIT_BLOCKS):
-                nc.tensor.matmul(
-                    out=total[:, k, :],
-                    lhsT=term[:, k * P : (k + 1) * P],
-                    rhs=ident[:],
-                    is_transpose=True,
-                    start=(first and k == 0),
-                    stop=(last and k == UNIT_BLOCKS - 1),
-                )
+        def add_block(total, term, k, first, last):
+            nc.tensor.matmul(
+                out=total[:, k, :],
+                lhsT=term[:, k * P : (k + 1) * P],
+                rhs=ident[:],
+                is_transpose=True,
+                start=(first and k == 0),
+                stop=(last and k == UNIT_BLOCKS - 1),
+            )
 
         totals = {}
 
@@ -216,10 +215,12 @@ def tile_plelayer_pa_e_kernel(
             if e == 0 and s != SHARED:
                 totals["task"] = psum_sum.tile([P, UNIT_BLOCKS, P], F32, name="task_total", tag="total")
             terms = terms_of[n]
-            add_term(totals["share"], terms[0], s == SHARED and e == 0, s == TASKS - 1 and e == EXPERTS - 1)
-            if s != SHARED:
-                add_term(totals["task"], terms[1], e == 0, False)
-                add_term(totals["task"], terms[2], False, e == EXPERTS - 1)
+            for k in range(UNIT_BLOCKS):
+                if s != SHARED:
+                    add_block(totals["task"], terms[1], k, e == 0, False)
+                add_block(totals["share"], terms[0], k, s == SHARED and e == 0, s == TASKS - 1 and e == EXPERTS - 1)
+                if s != SHARED:
+                    add_block(totals["task"], terms[2], k, False, e == EXPERTS - 1)
 
         def leave_psum(total):
             turned_in = out_pool.tile([P, UNIT_BLOCKS, P], F32, name="turned_in", bufs=3)

@@ -36,6 +36,7 @@ STEPS = ROUNDS * EXPERTS
 PASS_LEAD = 12
 GATE_LEAD = 2
 STORE_LAG = 2
+VECTOR_GATES_EVERY = 4
 WORD_PIECES = 4
 
 FLOPS = 2 * BATCH * D * COLS * SOURCES
@@ -49,7 +50,7 @@ def tile_plelayer_pa_e_kernel(
         ctx.enter_context(tc.manual_schedule())
         keep = ctx.enter_context(tc.tile_pool(name="keep", bufs=1))
         pre_pool = ctx.enter_context(tc.tile_pool(name="pre", bufs=1))
-        term_pool = ctx.enter_context(tc.tile_pool(name="term", bufs=12))
+        term_pool = ctx.enter_context(tc.tile_pool(name="term", bufs=10))
         out_pool = ctx.enter_context(tc.tile_pool(name="outp", bufs=2))
         psum_acc = ctx.enter_context(tc.psum_pool(name="psum_acc", bufs=3))
         psum_sum = ctx.enter_context(tc.psum_pool(name="psum_sum", bufs=3))
@@ -169,31 +170,45 @@ def tile_plelayer_pa_e_kernel(
                 op=ALU.add,
             )
 
-        def gated(pre, e, gate_column, number):
+        def gated(pre, e, gate_column, on_vector):
             term = term_pool.tile([P, UNITS], F32, name="term")
-            if number % 2 == 0:
-                nc.scalar.activation(out=term[:], in_=pre[:, e, :], func=ACT.Relu, scale=gate_column)
-            else:
+            if on_vector:
                 nc.vector.tensor_scalar(
                     out=term[:], in0=pre[:, e, :], scalar1=gate_column, scalar2=0.0, op0=ALU.mult, op1=ALU.max
                 )
+            else:
+                nc.scalar.activation(out=term[:], in_=pre[:, e, :], func=ACT.Relu, scale=gate_column)
             return term
 
         terms_of = {}
+        shared_part_of = {}
 
         def gate_step(n):
             r, e = divmod(n, EXPERTS)
             h, s = row_tile_of(r), source_of(r)
             j = s * EXPERTS + e
-            for_share = gated(pre_of[r], e, gate_share[:, h, j : j + 1], n)
             if s == SHARED:
-                terms_of[n] = [for_share]
+                nc.vector.tensor_scalar_max(out=pre_of[r][:, e, :], in0=pre_of[r][:, e, :], scalar1=0.0)
+                terms_of[n] = [gated(pre_of[r], e, gate_share[:, h, j : j + 1], False)]
             else:
                 g = s * TASK_GATES + e
-                shared_pre = pre_of[h * SOURCES]
-                own = gated(pre_of[r], e, gate_task[:, h, g : g + 1], n + 1)
-                shared = gated(shared_pre, e, gate_task[:, h, g + EXPERTS : g + EXPERTS + 1], n + 2)
-                terms_of[n] = [for_share, own, shared]
+                for_share = gated(pre_of[r], e, gate_share[:, h, j : j + 1], n % VECTOR_GATES_EVERY == 0)
+                for_task = gated(pre_of[r], e, gate_task[:, h, g : g + 1], False)
+                terms_of[n] = [for_share, for_task]
+                shared_relu = pre_of[h * SOURCES][:, e, :]
+                shared_gate = gate_task[:, h, g + EXPERTS : g + EXPERTS + 1]
+                if e == 0:
+                    shared_part_of[r] = out_pool.tile([P, UNITS], F32, name="shared_part", bufs=3)
+                    nc.vector.tensor_scalar_mul(out=shared_part_of[r][:], in0=shared_relu, scalar1=shared_gate)
+                else:
+                    nc.vector.scalar_tensor_tensor(
+                        out=shared_part_of[r][:],
+                        in0=shared_relu,
+                        scalar=shared_gate,
+                        in1=shared_part_of[r][:],
+                        op0=ALU.mult,
+                        op1=ALU.add,
+                    )
 
         def add_block(total, term, k, first, last):
             nc.tensor.matmul(
@@ -216,23 +231,29 @@ def tile_plelayer_pa_e_kernel(
                 totals["task"] = psum_sum.tile([P, UNIT_BLOCKS, P], F32, name="task_total", tag="total")
             terms = terms_of[n]
             for k in range(UNIT_BLOCKS):
-                if s != SHARED:
-                    add_block(totals["task"], terms[1], k, e == 0, False)
                 add_block(totals["share"], terms[0], k, s == SHARED and e == 0, s == TASKS - 1 and e == EXPERTS - 1)
                 if s != SHARED:
-                    add_block(totals["task"], terms[2], k, False, e == EXPERTS - 1)
+                    add_block(totals["task"], terms[1], k, e == 0, e == EXPERTS - 1)
 
-        def leave_psum(total):
+        def leave_psum(total, on_vector):
             turned_in = out_pool.tile([P, UNIT_BLOCKS, P], F32, name="turned_in", bufs=3)
-            nc.scalar.copy(out=turned_in[:], in_=total[:])
+            if on_vector:
+                nc.vector.tensor_copy(out=turned_in[:], in_=total[:])
+            else:
+                nc.scalar.copy(out=turned_in[:], in_=total[:])
             return turned_in
 
-        def turn_and_store(turned_in, rows):
+        def turn_and_store(turned_in, shared_part, rows):
             turned = psum_turn.tile([P, UNIT_BLOCKS, P], F32, name="turned", tag="turn")
             for k in range(UNIT_BLOCKS):
                 nc.tensor.transpose(turned[:, k, :], turned_in[:, k, :], ident[:])
             result = out_pool.tile([P, UNITS], F32, name="result")
-            nc.vector.tensor_copy(out=result[:], in_=turned[:].rearrange("p k u -> p (k u)"))
+            if shared_part is None:
+                nc.vector.tensor_copy(out=result[:], in_=turned[:].rearrange("p k u -> p (k u)"))
+            else:
+                nc.vector.tensor_tensor(
+                    out=result[:], in0=turned[:].rearrange("p k u -> p (k u)"), in1=shared_part[:], op=ALU.add
+                )
             nc.sync.dma_start(out=rows, in_=result[:])
 
         for q in range(PASS_LEAD):
@@ -250,8 +271,10 @@ def tile_plelayer_pa_e_kernel(
                 r, e = divmod(n, EXPERTS)
                 h, s = row_tile_of(r), source_of(r)
                 if e == EXPERTS - 1 and s != SHARED:
-                    leaving[n + STORE_LAG] = [(leave_psum(totals["task"]), out_0[s, h * P : (h + 1) * P, :])]
+                    leaving[n + STORE_LAG] = [
+                        (leave_psum(totals["task"], False), shared_part_of[r], out_0[s, h * P : (h + 1) * P, :])
+                    ]
                 if e == EXPERTS - 1 and s == TASKS - 1:
-                    leaving[n + STORE_LAG].append((leave_psum(totals["share"]), out_1[h * P : (h + 1) * P, :]))
-            for turned_in, rows in leaving.get(n, []):
-                turn_and_store(turned_in, rows)
+                    leaving[n + STORE_LAG].append((leave_psum(totals["share"], True), None, out_1[h * P : (h + 1) * P, :]))
+            for turned_in, shared_part, rows in leaving.get(n, []):
+                turn_and_store(turned_in, shared_part, rows)

@@ -37,6 +37,7 @@ PASS_LEAD = 12
 GATE_LEAD = 2
 STORE_LAG = 2
 VECTOR_GATES_EVERY = 4
+OPEN_ROWS = 4
 WORD_PIECES = 4
 
 FLOPS = 2 * BATCH * D * COLS * SOURCES
@@ -164,9 +165,11 @@ def tile_plelayer_pa_e_kernel(
                 stop=True,
             )
             nc.vector.tensor_tensor(
-                out=pre_of[r][:, :, c * PASS_UNITS : (c + 1) * PASS_UNITS],
-                in0=acc[:].rearrange("p (u e) -> p e u", e=EXPERTS),
-                in1=bias_all[:, s, c * PASS_COLS : (c + 1) * PASS_COLS].rearrange("p (u e) -> p e u", e=EXPERTS),
+                out=pre_of[r][:, :, c * PASS_UNITS : (c + 1) * PASS_UNITS].rearrange("p (g e) u -> p g u e", e=OPEN_ROWS),
+                in0=acc[:].rearrange("p (u g e) -> p g u e", u=PASS_UNITS, e=OPEN_ROWS),
+                in1=bias_all[:, s, c * PASS_COLS : (c + 1) * PASS_COLS].rearrange(
+                    "p (u g e) -> p g u e", u=PASS_UNITS, e=OPEN_ROWS
+                ),
                 op=ALU.add,
             )
 

@@ -15,6 +15,7 @@ ACT = mybir.ActivationFunctionType
 AXIS = mybir.AxisListType
 
 P = 128
+PACK = 4
 TASKS = 4
 BATCH = 256
 ROW_TILES = BATCH // P
@@ -30,17 +31,27 @@ PASSES = COLS // PASS_COLS
 UNIT_BLOCKS = UNITS // P
 TASK_GATES = 2 * EXPERTS
 SHARE_GATES = SOURCES * EXPERTS
+SCALE_ROWS = 4
+QUADRANTS = 4
 
 ROUNDS = ROW_TILES * SOURCES
 STEPS = ROUNDS * EXPERTS
+assert PASSES == EXPERTS
 PASS_LEAD = 12
 GATE_LEAD = 2
 STORE_LAG = 2
-VECTOR_GATES_EVERY = 4
-OPEN_ROWS = 4
-WORD_PIECES = 4
+ROWS_IN_TURN = 4
+LOAD_PIECES = 4
 
 FLOPS = 2 * BATCH * D * COLS * SOURCES
+
+
+def row_tile_of(r):
+    return r // SOURCES
+
+
+def source_of(r):
+    return SHARED if r % SOURCES == 0 else r % SOURCES - 1
 
 
 def tile_plelayer_pa_e_kernel(
@@ -50,9 +61,7 @@ def tile_plelayer_pa_e_kernel(
     with ExitStack() as ctx:
         ctx.enter_context(tc.manual_schedule())
         keep = ctx.enter_context(tc.tile_pool(name="keep", bufs=1))
-        pre_pool = ctx.enter_context(tc.tile_pool(name="pre", bufs=1))
-        term_pool = ctx.enter_context(tc.tile_pool(name="term", bufs=10))
-        out_pool = ctx.enter_context(tc.tile_pool(name="outp", bufs=2))
+        work = ctx.enter_context(tc.tile_pool(name="work", bufs=1))
         psum_acc = ctx.enter_context(tc.psum_pool(name="psum_acc", bufs=3))
         psum_sum = ctx.enter_context(tc.psum_pool(name="psum_sum", bufs=3))
         psum_turn = ctx.enter_context(tc.psum_pool(name="psum_turn", bufs=2))
@@ -63,34 +72,35 @@ def tile_plelayer_pa_e_kernel(
         x_sb = keep.tile([P, ROW_TILES, D], BF16, name="x_sb")
         nc.sync.dma_start(out=x_sb[:], in_=x.rearrange("(h p) d -> p h d", p=P))
 
-        pre_task = keep.tile([P, ROW_TILES, TASKS * TASK_GATES], BF16, name="pre_task")
+        logits_task = keep.tile([P, ROW_TILES, TASKS * TASK_GATES], BF16, name="logits_task")
         for h in range(ROW_TILES):
             nc.scalar.dma_start(
-                out=pre_task[:, h, :].rearrange("p (t g) -> p t g", g=TASK_GATES),
+                out=logits_task[:, h, :].rearrange("p (t g) -> p t g", g=TASK_GATES),
                 in_=gate_pre0[:, h * P : (h + 1) * P, :].rearrange("t p g -> p t g"),
             )
-        pre_share = keep.tile([P, ROW_TILES, SHARE_GATES], BF16, name="pre_share")
-        nc.scalar.dma_start(out=pre_share[:], in_=sgate_pre.rearrange("(h p) g -> p h g", p=P))
-        gb_task = keep.tile([P, TASKS * TASK_GATES], BF16, name="gb_task")
-        nc.scalar.dma_start(out=gb_task[:], in_=gb0.rearrange("t g -> (t g)").partition_broadcast(P))
-        gb_share = keep.tile([P, SHARE_GATES], BF16, name="gb_share")
-        nc.scalar.dma_start(out=gb_share[:], in_=gbs.partition_broadcast(P))
+        logits_share = keep.tile([P, ROW_TILES, SHARE_GATES], BF16, name="logits_share")
+        nc.scalar.dma_start(out=logits_share[:], in_=sgate_pre.rearrange("(h p) g -> p h g", p=P))
+        gate_bias_task = keep.tile([P, TASKS * TASK_GATES], BF16, name="gate_bias_task")
+        nc.scalar.dma_start(out=gate_bias_task[:], in_=gb0.rearrange("t g -> (t g)").partition_broadcast(P))
+        gate_bias_share = keep.tile([P, SHARE_GATES], BF16, name="gate_bias_share")
+        nc.scalar.dma_start(out=gate_bias_share[:], in_=gbs.partition_broadcast(P))
 
         words = keep.tile([P, SOURCES, 2 * COLS], U8, name="words", align_bytes=64)
         planes = keep.tile([P, SOURCES, COLS], U8, name="planes", align_bytes=64)
         bias_all = keep.tile([P, SOURCES, COLS], BF16, name="bias_all")
-        piece = 2 * COLS // WORD_PIECES
-        for s in (SHARED, 0, 1, 2, 3):
+        piece = 2 * COLS // LOAD_PIECES
+        for r in range(SOURCES):
+            s = source_of(r)
             src_words = ews0_words[0] if s == SHARED else ew0_words[s]
             src_scales = ews0_scales[0] if s == SHARED else ew0_scales[s]
             src_bias = ebs0 if s == SHARED else eb0[s]
             nc.vector.memset(planes[:, s, :].bitcast(I32), 0)
-            for quad in range(4):
+            for quad in range(QUADRANTS):
                 nc.sync.dma_start(
-                    out=planes[32 * quad : 32 * quad + 4, s, :].bitcast(I32),
-                    in_=src_scales[4 * quad : 4 * quad + 4, :].bitcast(I32),
+                    out=planes[32 * quad : 32 * quad + SCALE_ROWS, s, :].bitcast(I32),
+                    in_=src_scales[SCALE_ROWS * quad : SCALE_ROWS * (quad + 1), :].bitcast(I32),
                 )
-            for w in range(WORD_PIECES):
+            for w in range(LOAD_PIECES):
                 nc.sync.dma_start(
                     out=words[:, s, w * piece : (w + 1) * piece].bitcast(I32),
                     in_=src_words[:, w * piece : (w + 1) * piece].bitcast(I32),
@@ -99,61 +109,54 @@ def tile_plelayer_pa_e_kernel(
                 out=bias_all[:, s, :], in_=src_bias.rearrange("u e -> (u e)").partition_broadcast(P)
             )
 
-        x_turn = psum_turn.tile([P, ROW_TILES, 2, P], F32, name="x_turn", tag="turn")
+        x_turned = psum_turn.tile([P, ROW_TILES, 2, P], F32, name="x_turned", tag="turn")
         for h in range(ROW_TILES):
-            x_words = x_sb[:, h, :].bitcast(F32)
+            x_pairs = x_sb[:, h, :].bitcast(F32)
             for v in range(2):
-                nc.tensor.transpose(x_turn[:, h, v, :], x_words[:, v : D // 2 : 2], ident[:])
-        x_grouped = keep.tile([P, BATCH * 4], BF16, name="x_grouped", align_bytes=64)
+                nc.tensor.transpose(x_turned[:, h, v, :], x_pairs[:, v : D // 2 : 2], ident[:])
+        x_grouped = keep.tile([P, BATCH * PACK], BF16, name="x_grouped", align_bytes=64)
         nc.vector.tensor_copy(
             out=x_grouped[:].bitcast(F32).rearrange("p (h b v) -> p h b v", h=ROW_TILES, v=2),
-            in_=x_turn[:].rearrange("p h v b -> p h b v"),
+            in_=x_turned[:].rearrange("p h v b -> p h b v"),
         )
         x_codes = keep.tile([P, BATCH], U32, name="x_codes", align_bytes=64)
         x_scales = keep.tile([P, BATCH], U8, name="x_scales", align_bytes=64)
         nc.vector.quantize_mx(out=x_codes[:].bitcast(FP8X4), scales=x_scales[:], in_=x_grouped[:])
 
-        def softmax_groups(pre, bias, width, name):
-            entries = pre.shape[2]
-            groups = ROW_TILES * entries // width
+        def softmax_runs(logits, bias, width, name):
+            entries = logits.shape[2]
+            runs = ROW_TILES * entries // width
             gate = keep.tile([P, ROW_TILES, entries], F32, name=name)
-            top = keep.tile([P, groups], F32, name=name + "_top")
-            total = keep.tile([P, groups], F32, name=name + "_total")
-            grouped = gate[:].rearrange("p h (n g) -> p (h n) g", g=width)
+            top = keep.tile([P, runs], F32, name=name + "_top")
+            norm = keep.tile([P, runs], F32, name=name + "_norm")
+            by_run = gate[:].rearrange("p h (n g) -> p (h n) g", g=width)
             nc.vector.tensor_tensor(
-                out=gate[:], in0=pre, in1=bias.unsqueeze(1).to_broadcast([P, ROW_TILES, entries]), op=ALU.add
+                out=gate[:], in0=logits, in1=bias.unsqueeze(1).to_broadcast([P, ROW_TILES, entries]), op=ALU.add
             )
-            nc.vector.tensor_reduce(out=top[:], in_=grouped, axis=AXIS.X, op=ALU.max)
+            nc.vector.tensor_reduce(out=top[:], in_=by_run, axis=AXIS.X, op=ALU.max)
             nc.vector.tensor_tensor(
-                out=grouped, in0=grouped, in1=top[:].unsqueeze(2).to_broadcast([P, groups, width]), op=ALU.subtract
+                out=by_run, in0=by_run, in1=top[:].unsqueeze(2).to_broadcast([P, runs, width]), op=ALU.subtract
             )
             nc.scalar.activation(out=gate[:], in_=gate[:], func=ACT.Exp)
-            nc.vector.tensor_reduce(out=total[:], in_=grouped, axis=AXIS.X, op=ALU.add)
-            nc.vector.reciprocal(out=total[:], in_=total[:])
+            nc.vector.tensor_reduce(out=norm[:], in_=by_run, axis=AXIS.X, op=ALU.add)
+            nc.vector.reciprocal(out=norm[:], in_=norm[:])
             nc.vector.tensor_tensor(
-                out=grouped, in0=grouped, in1=total[:].unsqueeze(2).to_broadcast([P, groups, width]), op=ALU.mult
+                out=by_run, in0=by_run, in1=norm[:].unsqueeze(2).to_broadcast([P, runs, width]), op=ALU.mult
             )
             return gate
 
-        gate_task = softmax_groups(pre_task[:], gb_task[:], TASK_GATES, "gate_task")
-        gate_share = softmax_groups(pre_share[:], gb_share[:], SHARE_GATES, "gate_share")
-
-        def row_tile_of(r):
-            return r // SOURCES
-
-        def source_of(r):
-            return SHARED if r % SOURCES == 0 else r % SOURCES - 1
+        gate_task = softmax_runs(logits_task[:], gate_bias_task[:], TASK_GATES, "gate_task")
+        gate_share = softmax_runs(logits_share[:], gate_bias_share[:], SHARE_GATES, "gate_share")
 
         pre_of = {}
 
         def issue_pass(q):
             r, c = divmod(q, PASSES)
             h, s = row_tile_of(r), source_of(r)
-            if c == 0:
-                if s == SHARED:
-                    pre_of[r] = pre_pool.tile([P, EXPERTS, UNITS], F32, name="pre_shared", tag="shared", bufs=2)
-                else:
-                    pre_of[r] = pre_pool.tile([P, EXPERTS, UNITS], F32, name="pre_own", tag="own", bufs=3)
+            if c == 0 and s == SHARED:
+                pre_of[r] = work.tile([P, EXPERTS, UNITS], F32, name="pre_shared", bufs=2)
+            if c == 0 and s != SHARED:
+                pre_of[r] = work.tile([P, EXPERTS, UNITS], F32, name="pre_own", bufs=3)
             acc = psum_acc.tile([P, PASS_COLS], F32, name="acc")
             nc.tensor.matmul_mx(
                 out=acc[:],
@@ -165,22 +168,19 @@ def tile_plelayer_pa_e_kernel(
                 stop=True,
             )
             nc.vector.tensor_tensor(
-                out=pre_of[r][:, :, c * PASS_UNITS : (c + 1) * PASS_UNITS].rearrange("p (g e) u -> p g u e", e=OPEN_ROWS),
-                in0=acc[:].rearrange("p (u g e) -> p g u e", u=PASS_UNITS, e=OPEN_ROWS),
+                out=pre_of[r][:, :, c * PASS_UNITS : (c + 1) * PASS_UNITS].rearrange(
+                    "p (g e) u -> p g u e", e=ROWS_IN_TURN
+                ),
+                in0=acc[:].rearrange("p (u g e) -> p g u e", u=PASS_UNITS, e=ROWS_IN_TURN),
                 in1=bias_all[:, s, c * PASS_COLS : (c + 1) * PASS_COLS].rearrange(
-                    "p (u g e) -> p g u e", u=PASS_UNITS, e=OPEN_ROWS
+                    "p (u g e) -> p g u e", u=PASS_UNITS, e=ROWS_IN_TURN
                 ),
                 op=ALU.add,
             )
 
-        def gated(pre, e, gate_column, on_vector):
-            term = term_pool.tile([P, UNITS], F32, name="term")
-            if on_vector:
-                nc.vector.tensor_scalar(
-                    out=term[:], in0=pre[:, e, :], scalar1=gate_column, scalar2=0.0, op0=ALU.mult, op1=ALU.max
-                )
-            else:
-                nc.scalar.activation(out=term[:], in_=pre[:, e, :], func=ACT.Relu, scale=gate_column)
+        def gated(pre, e, gate_column):
+            term = work.tile([P, UNITS], F32, name="term", bufs=10)
+            nc.scalar.activation(out=term[:], in_=pre[:, e, :], func=ACT.Relu, scale=gate_column)
             return term
 
         terms_of = {}
@@ -192,16 +192,17 @@ def tile_plelayer_pa_e_kernel(
             j = s * EXPERTS + e
             if s == SHARED:
                 nc.vector.tensor_scalar_max(out=pre_of[r][:, e, :], in0=pre_of[r][:, e, :], scalar1=0.0)
-                terms_of[n] = [gated(pre_of[r], e, gate_share[:, h, j : j + 1], False)]
+                terms_of[n] = [gated(pre_of[r], e, gate_share[:, h, j : j + 1])]
             else:
                 g = s * TASK_GATES + e
-                for_share = gated(pre_of[r], e, gate_share[:, h, j : j + 1], n % VECTOR_GATES_EVERY == 0)
-                for_task = gated(pre_of[r], e, gate_task[:, h, g : g + 1], False)
-                terms_of[n] = [for_share, for_task]
+                terms_of[n] = [
+                    gated(pre_of[r], e, gate_share[:, h, j : j + 1]),
+                    gated(pre_of[r], e, gate_task[:, h, g : g + 1]),
+                ]
                 shared_relu = pre_of[h * SOURCES][:, e, :]
                 shared_gate = gate_task[:, h, g + EXPERTS : g + EXPERTS + 1]
                 if e == 0:
-                    shared_part_of[r] = out_pool.tile([P, UNITS], F32, name="shared_part", bufs=3)
+                    shared_part_of[r] = work.tile([P, UNITS], F32, name="shared_part", bufs=3)
                     nc.vector.tensor_scalar_mul(out=shared_part_of[r][:], in0=shared_relu, scalar1=shared_gate)
                 else:
                     nc.vector.scalar_tensor_tensor(
@@ -239,7 +240,7 @@ def tile_plelayer_pa_e_kernel(
                     add_block(totals["task"], terms[1], k, e == 0, e == EXPERTS - 1)
 
         def leave_psum(total, on_vector):
-            turned_in = out_pool.tile([P, UNIT_BLOCKS, P], F32, name="turned_in", bufs=3)
+            turned_in = work.tile([P, UNIT_BLOCKS, P], F32, name="turned_in", bufs=3)
             if on_vector:
                 nc.vector.tensor_copy(out=turned_in[:], in_=total[:])
             else:
@@ -250,7 +251,7 @@ def tile_plelayer_pa_e_kernel(
             turned = psum_turn.tile([P, UNIT_BLOCKS, P], F32, name="turned", tag="turn")
             for k in range(UNIT_BLOCKS):
                 nc.tensor.transpose(turned[:, k, :], turned_in[:, k, :], ident[:])
-            result = out_pool.tile([P, UNITS], F32, name="result")
+            result = work.tile([P, UNITS], F32, name="result", bufs=2)
             if shared_part is None:
                 nc.vector.tensor_copy(out=result[:], in_=turned[:].rearrange("p k u -> p (k u)"))
             else:
@@ -259,10 +260,12 @@ def tile_plelayer_pa_e_kernel(
                 )
             nc.sync.dma_start(out=rows, in_=result[:])
 
-        for q in range(PASS_LEAD):
+        for q in range(PASSES):
             issue_pass(q)
         for n in range(GATE_LEAD):
             gate_step(n)
+        for q in range(PASSES, PASS_LEAD):
+            issue_pass(q)
         leaving = {}
         for n in range(STEPS + STORE_LAG):
             if n + GATE_LEAD < STEPS:

@@ -214,12 +214,12 @@ def tile_plelayer_pa_e_kernel(
                         op1=ALU.add,
                     )
 
-        def add_block(total, term, k, first, last):
+        def add_block(total, term, k, first, last, as_transpose=True):
             nc.tensor.matmul(
                 out=total[:, k, :],
                 lhsT=term[:, k * P : (k + 1) * P],
                 rhs=ident[:],
-                is_transpose=True,
+                is_transpose=as_transpose,
                 start=(first and k == 0),
                 stop=(last and k == UNIT_BLOCKS - 1),
             )
@@ -235,7 +235,9 @@ def tile_plelayer_pa_e_kernel(
                 totals["task"] = psum_sum.tile([P, UNIT_BLOCKS, P], F32, name="task_total", tag="total")
             terms = terms_of[n]
             for k in range(UNIT_BLOCKS):
-                add_block(totals["share"], terms[0], k, s == SHARED and e == 0, s == TASKS - 1 and e == EXPERTS - 1)
+                add_block(
+                    totals["share"], terms[0], k, s == SHARED and e == 0, s == TASKS - 1 and e == EXPERTS - 1, k != 0
+                )
                 if s != SHARED:
                     add_block(totals["task"], terms[1], k, e == 0, e == EXPERTS - 1)
 

@@ -70,7 +70,7 @@ def tile_plelayer_pa_e_kernel(
         make_identity(nc, ident[:])
 
         x_sb = keep.tile([P, ROW_TILES, D], BF16, name="x_sb")
-        nc.sync.dma_start(out=x_sb[:], in_=x.rearrange("(h p) d -> p h d", p=P))
+        nc.sync.dma_start(out=x_sb[:, 0, :], in_=x[0:P, :])
 
         logits_task = keep.tile([P, ROW_TILES, TASKS * TASK_GATES], BF16, name="logits_task")
         for h in range(ROW_TILES):
@@ -84,6 +84,8 @@ def tile_plelayer_pa_e_kernel(
         nc.scalar.dma_start(out=gate_bias_task[:], in_=gb0.rearrange("t g -> (t g)").partition_broadcast(P))
         gate_bias_share = keep.tile([P, SHARE_GATES], BF16, name="gate_bias_share")
         nc.scalar.dma_start(out=gate_bias_share[:], in_=gbs.partition_broadcast(P))
+        warm = keep.tile([P, 1], F32, name="warm")
+        nc.scalar.activation(out=warm[:], in_=ident[:, 0:1], func=ACT.Exp)
 
         words = keep.tile([P, SOURCES, 2 * COLS], U8, name="words", align_bytes=64)
         planes = keep.tile([P, SOURCES, COLS], U8, name="planes", align_bytes=64)
@@ -100,35 +102,45 @@ def tile_plelayer_pa_e_kernel(
                     out=planes[32 * quad : 32 * quad + SCALE_ROWS, s, :].bitcast(I32),
                     in_=src_scales[SCALE_ROWS * quad : SCALE_ROWS * (quad + 1), :].bitcast(I32),
                 )
+            flat_bias = src_bias.rearrange("u e -> (u e)")
             for w in range(LOAD_PIECES):
                 nc.sync.dma_start(
                     out=words[:, s, w * piece : (w + 1) * piece].bitcast(I32),
                     in_=src_words[:, w * piece : (w + 1) * piece].bitcast(I32),
                 )
-            nc.gpsimd.dma_start(
-                out=bias_all[:, s, :], in_=src_bias.rearrange("u e -> (u e)").partition_broadcast(P)
-            )
+            if r == 0:
+                nc.sync.dma_start(out=x_sb[:, 1, :], in_=x[P : 2 * P, :])
+            bias_pieces = LOAD_PIECES if r == 0 else 1
+            for w in range(bias_pieces):
+                columns = slice(w * COLS // bias_pieces, (w + 1) * COLS // bias_pieces)
+                nc.gpsimd.dma_start(out=bias_all[:, s, columns], in_=flat_bias[columns].partition_broadcast(P))
 
-        x_turned = psum_turn.tile([P, ROW_TILES, 2, P], F32, name="x_turned", tag="turn")
-        for h in range(ROW_TILES):
-            x_pairs = x_sb[:, h, :].bitcast(F32)
-            for v in range(2):
-                nc.tensor.transpose(x_turned[:, h, v, :], x_pairs[:, v : D // 2 : 2], ident[:])
         x_grouped = keep.tile([P, BATCH * PACK], BF16, name="x_grouped", align_bytes=64)
-        nc.vector.tensor_copy(
-            out=x_grouped[:].bitcast(F32).rearrange("p (h b v) -> p h b v", h=ROW_TILES, v=2),
-            in_=x_turned[:].rearrange("p h v b -> p h b v"),
-        )
         x_codes = keep.tile([P, BATCH], U32, name="x_codes", align_bytes=64)
         x_scales = keep.tile([P, BATCH], U8, name="x_scales", align_bytes=64)
-        nc.vector.quantize_mx(out=x_codes[:].bitcast(FP8X4), scales=x_scales[:], in_=x_grouped[:])
 
-        def softmax_runs(logits, bias, width, name):
+        def group_rows(h):
+            x_turned = psum_turn.tile([P, 2, P], F32, name="x_turned", tag="turn")
+            x_pairs = x_sb[:, h, :].bitcast(F32)
+            for v in range(2):
+                nc.tensor.transpose(x_turned[:, v, :], x_pairs[:, v : D // 2 : 2], ident[:])
+            nc.vector.tensor_copy(
+                out=x_grouped[:, h * P * PACK : (h + 1) * P * PACK].bitcast(F32).rearrange("p (b v) -> p b v", v=2),
+                in_=x_turned[:].rearrange("p v b -> p b v"),
+            )
+
+        def quantise_rows(h):
+            nc.vector.quantize_mx(
+                out=x_codes[:, h * P : (h + 1) * P].bitcast(FP8X4),
+                scales=x_scales[:, h * P : (h + 1) * P],
+                in_=x_grouped[:, h * P * PACK : (h + 1) * P * PACK],
+            )
+
+        def softmax_open(logits, bias, width, name):
             entries = logits.shape[2]
             runs = ROW_TILES * entries // width
             gate = keep.tile([P, ROW_TILES, entries], F32, name=name)
             top = keep.tile([P, runs], F32, name=name + "_top")
-            norm = keep.tile([P, runs], F32, name=name + "_norm")
             by_run = gate[:].rearrange("p h (n g) -> p (h n) g", g=width)
             nc.vector.tensor_tensor(
                 out=gate[:], in0=logits, in1=bias.unsqueeze(1).to_broadcast([P, ROW_TILES, entries]), op=ALU.add
@@ -138,15 +150,24 @@ def tile_plelayer_pa_e_kernel(
                 out=by_run, in0=by_run, in1=top[:].unsqueeze(2).to_broadcast([P, runs, width]), op=ALU.subtract
             )
             nc.scalar.activation(out=gate[:], in_=gate[:], func=ACT.Exp)
+            return gate
+
+        def softmax_close(gate, width, name):
+            runs = ROW_TILES * gate.shape[2] // width
+            norm = keep.tile([P, runs], F32, name=name + "_norm")
+            by_run = gate[:].rearrange("p h (n g) -> p (h n) g", g=width)
             nc.vector.tensor_reduce(out=norm[:], in_=by_run, axis=AXIS.X, op=ALU.add)
             nc.vector.reciprocal(out=norm[:], in_=norm[:])
             nc.vector.tensor_tensor(
                 out=by_run, in0=by_run, in1=norm[:].unsqueeze(2).to_broadcast([P, runs, width]), op=ALU.mult
             )
-            return gate
 
-        gate_task = softmax_runs(logits_task[:], gate_bias_task[:], TASK_GATES, "gate_task")
-        gate_share = softmax_runs(logits_share[:], gate_bias_share[:], SHARE_GATES, "gate_share")
+        gate_task = softmax_open(logits_task[:], gate_bias_task[:], TASK_GATES, "gate_task")
+        gate_share = softmax_open(logits_share[:], gate_bias_share[:], SHARE_GATES, "gate_share")
+        group_rows(0)
+        softmax_close(gate_task, TASK_GATES, "gate_task")
+        quantise_rows(0)
+        softmax_close(gate_share, SHARE_GATES, "gate_share")
 
         pre_of = {}
 
@@ -178,9 +199,14 @@ def tile_plelayer_pa_e_kernel(
                 op=ALU.add,
             )
 
-        def gated(pre, e, gate_column):
+        def gated(pre, e, gate_column, on_vector=False):
             term = work.tile([P, UNITS], F32, name="term", bufs=10)
-            nc.scalar.activation(out=term[:], in_=pre[:, e, :], func=ACT.Relu, scale=gate_column)
+            if on_vector:
+                nc.vector.tensor_scalar(
+                    out=term[:], in0=pre[:, e, :], scalar1=gate_column, scalar2=0.0, op0=ALU.mult, op1=ALU.max
+                )
+            else:
+                nc.scalar.activation(out=term[:], in_=pre[:, e, :], func=ACT.Relu, scale=gate_column)
             return term
 
         terms_of = {}
@@ -191,13 +217,16 @@ def tile_plelayer_pa_e_kernel(
             h, s = row_tile_of(r), source_of(r)
             j = s * EXPERTS + e
             if s == SHARED:
-                nc.vector.tensor_scalar_max(out=pre_of[r][:, e, :], in0=pre_of[r][:, e, :], scalar1=0.0)
                 terms_of[n] = [gated(pre_of[r], e, gate_share[:, h, j : j + 1])]
+                if e % 2 == 0:
+                    nc.vector.tensor_scalar_max(out=pre_of[r][:, e, :], in0=pre_of[r][:, e, :], scalar1=0.0)
+                else:
+                    nc.scalar.activation(out=pre_of[r][:, e, :], in_=pre_of[r][:, e, :], func=ACT.Relu)
             else:
                 g = s * TASK_GATES + e
                 terms_of[n] = [
                     gated(pre_of[r], e, gate_share[:, h, j : j + 1]),
-                    gated(pre_of[r], e, gate_task[:, h, g : g + 1]),
+                    gated(pre_of[r], e, gate_task[:, h, g : g + 1], n - GATE_LEAD + PASS_LEAD >= STEPS),
                 ]
                 shared_relu = pre_of[h * SOURCES][:, e, :]
                 shared_gate = gate_task[:, h, g + EXPERTS : g + EXPERTS + 1]
@@ -255,7 +284,7 @@ def tile_plelayer_pa_e_kernel(
                 nc.tensor.transpose(turned[:, k, :], turned_in[:, k, :], ident[:])
             result = work.tile([P, UNITS], F32, name="result", bufs=2)
             if shared_part is None:
-                nc.vector.tensor_copy(out=result[:], in_=turned[:].rearrange("p k u -> p (k u)"))
+                nc.scalar.copy(out=result[:], in_=turned[:].rearrange("p k u -> p (k u)"))
             else:
                 nc.vector.tensor_tensor(
                     out=result[:], in0=turned[:].rearrange("p k u -> p (k u)"), in1=shared_part[:], op=ALU.add
@@ -270,6 +299,10 @@ def tile_plelayer_pa_e_kernel(
             issue_pass(q)
         leaving = {}
         for n in range(STEPS + STORE_LAG):
+            if n == 0:
+                group_rows(1)
+            if n == 1:
+                quantise_rows(1)
             if n + GATE_LEAD < STEPS:
                 gate_step(n + GATE_LEAD)
             if n + PASS_LEAD < STEPS:

from contextlib import ExitStack

import concourse.mybir as mybir
from concourse.masks import make_identity

F32 = mybir.dt.float32
BF16 = mybir.dt.bfloat16
I32 = mybir.dt.int32
U8 = mybir.dt.uint8
U32 = mybir.dt.uint32
FP8X4 = mybir.dt.float8_e4m3fn_x4
FP4X4 = mybir.dt.float4_e2m1fn_x4
ALU = mybir.AluOpType
ACT = mybir.ActivationFunctionType
AXIS = mybir.AxisListType

P = 128
PACK = 4
TASKS = 4
BATCH = 256
ROW_TILES = BATCH // P
D = 512
UNITS = 512
EXPERTS = 8
SOURCES = TASKS + 1
SHARED = TASKS
COLS = UNITS * EXPERTS
PASS_COLS = 512
PASS_UNITS = PASS_COLS // EXPERTS
PASSES = COLS // PASS_COLS
UNIT_BLOCKS = UNITS // P
TASK_GATES = 2 * EXPERTS
SHARE_GATES = SOURCES * EXPERTS
SCALE_ROWS = 4
QUADRANTS = 4

ROUNDS = ROW_TILES * SOURCES
STEPS = ROUNDS * EXPERTS
assert PASSES == EXPERTS
PASS_LEAD = 12
GATE_LEAD = 2
STORE_LAG = 2
ROWS_IN_TURN = 4
LOAD_PIECES = 4

FLOPS = 2 * BATCH * D * COLS * SOURCES


def row_tile_of(r):
    return r // SOURCES


def source_of(r):
    return SHARED if r % SOURCES == 0 else r % SOURCES - 1


def tile_plelayer_pa_e_kernel(
    tc, x, ews0_words, ews0_scales, ebs0, ew0_words, ew0_scales, eb0, gate_pre0, gb0, sgate_pre, gbs, out_0, out_1
):
    nc = tc.nc
    with ExitStack() as ctx:
        ctx.enter_context(tc.manual_schedule())
        keep = ctx.enter_context(tc.tile_pool(name="keep", bufs=1))
        work = ctx.enter_context(tc.tile_pool(name="work", bufs=1))
        psum_acc = ctx.enter_context(tc.psum_pool(name="psum_acc", bufs=3))
        psum_sum = ctx.enter_context(tc.psum_pool(name="psum_sum", bufs=3))
        psum_turn = ctx.enter_context(tc.psum_pool(name="psum_turn", bufs=2))

        ident = keep.tile([P, P], F32, name="ident")
        make_identity(nc, ident[:])

        x_sb = keep.tile([P, ROW_TILES, D], BF16, name="x_sb")
        nc.sync.dma_start(out=x_sb[:, 0, :], in_=x[0:P, :])

        logits_task = keep.tile([P, ROW_TILES, TASKS * TASK_GATES], BF16, name="logits_task")
        for h in range(ROW_TILES):
            nc.scalar.dma_start(
                out=logits_task[:, h, :].rearrange("p (t g) -> p t g", g=TASK_GATES),
                in_=gate_pre0[:, h * P : (h + 1) * P, :].rearrange("t p g -> p t g"),
            )
        logits_share = keep.tile([P, ROW_TILES, SHARE_GATES], BF16, name="logits_share")
        nc.scalar.dma_start(out=logits_share[:], in_=sgate_pre.rearrange("(h p) g -> p h g", p=P))
        gate_bias_task = keep.tile([P, TASKS * TASK_GATES], BF16, name="gate_bias_task")
        nc.scalar.dma_start(out=gate_bias_task[:], in_=gb0.rearrange("t g -> (t g)").partition_broadcast(P))
        gate_bias_share = keep.tile([P, SHARE_GATES], BF16, name="gate_bias_share")
        nc.scalar.dma_start(out=gate_bias_share[:], in_=gbs.partition_broadcast(P))
        warm = keep.tile([P, 1], F32, name="warm")
        nc.scalar.activation(out=warm[:], in_=ident[:, 0:1], func=ACT.Exp)

        words = keep.tile([P, SOURCES, 2 * COLS], U8, name="words", align_bytes=64)
        planes = keep.tile([P, SOURCES, COLS], U8, name="planes", align_bytes=64)
        bias_all = keep.tile([P, SOURCES, COLS], BF16, name="bias_all")
        piece = 2 * COLS // LOAD_PIECES
        for r in range(SOURCES):
            s = source_of(r)
            src_words = ews0_words[0] if s == SHARED else ew0_words[s]
            src_scales = ews0_scales[0] if s == SHARED else ew0_scales[s]
            src_bias = ebs0 if s == SHARED else eb0[s]
            nc.vector.memset(planes[:, s, :].bitcast(I32), 0)
            for quad in range(QUADRANTS):
                nc.sync.dma_start(
                    out=planes[32 * quad : 32 * quad + SCALE_ROWS, s, :].bitcast(I32),
                    in_=src_scales[SCALE_ROWS * quad : SCALE_ROWS * (quad + 1), :].bitcast(I32),
                )
            flat_bias = src_bias.rearrange("u e -> (u e)")
            for w in range(LOAD_PIECES):
                nc.sync.dma_start(
                    out=words[:, s, w * piece : (w + 1) * piece].bitcast(I32),
                    in_=src_words[:, w * piece : (w + 1) * piece].bitcast(I32),
                )
            if r == 0:
                nc.sync.dma_start(out=x_sb[:, 1, :], in_=x[P : 2 * P, :])
            bias_pieces = LOAD_PIECES if r == 0 else 1
            for w in range(bias_pieces):
                columns = slice(w * COLS // bias_pieces, (w + 1) * COLS // bias_pieces)
                nc.gpsimd.dma_start(out=bias_all[:, s, columns], in_=flat_bias[columns].partition_broadcast(P))

        x_grouped = keep.tile([P, BATCH * PACK], BF16, name="x_grouped", align_bytes=64)
        x_codes = keep.tile([P, BATCH], U32, name="x_codes", align_bytes=64)
        x_scales = keep.tile([P, BATCH], U8, name="x_scales", align_bytes=64)

        def group_rows(h):
            x_turned = psum_turn.tile([P, 2, P], F32, name="x_turned", tag="turn")
            x_pairs = x_sb[:, h, :].bitcast(F32)
            for v in range(2):
                nc.tensor.transpose(x_turned[:, v, :], x_pairs[:, v : D // 2 : 2], ident[:])
            nc.vector.tensor_copy(
                out=x_grouped[:, h * P * PACK : (h + 1) * P * PACK].bitcast(F32).rearrange("p (b v) -> p b v", v=2),
                in_=x_turned[:].rearrange("p v b -> p b v"),
            )

        def quantise_rows(h):
            nc.vector.quantize_mx(
                out=x_codes[:, h * P : (h + 1) * P].bitcast(FP8X4),
                scales=x_scales[:, h * P : (h + 1) * P],
                in_=x_grouped[:, h * P * PACK : (h + 1) * P * PACK],
            )

        def softmax_open(logits, bias, width, name):
            entries = logits.shape[2]
            runs = ROW_TILES * entries // width
            gate = keep.tile([P, ROW_TILES, entries], F32, name=name)
            top = keep.tile([P, runs], F32, name=name + "_top")
            by_run = gate[:].rearrange("p h (n g) -> p (h n) g", g=width)
            nc.vector.tensor_tensor(
                out=gate[:], in0=logits, in1=bias.unsqueeze(1).to_broadcast([P, ROW_TILES, entries]), op=ALU.add
            )
            nc.vector.tensor_reduce(out=top[:], in_=by_run, axis=AXIS.X, op=ALU.max)
            nc.vector.tensor_tensor(
                out=by_run, in0=by_run, in1=top[:].unsqueeze(2).to_broadcast([P, runs, width]), op=ALU.subtract
            )
            nc.scalar.activation(out=gate[:], in_=gate[:], func=ACT.Exp)
            return gate

        def softmax_close(gate, width, name):
            runs = ROW_TILES * gate.shape[2] // width
            norm = keep.tile([P, runs], F32, name=name + "_norm")
            by_run = gate[:].rearrange("p h (n g) -> p (h n) g", g=width)
            nc.vector.tensor_reduce(out=norm[:], in_=by_run, axis=AXIS.X, op=ALU.add)
            nc.vector.reciprocal(out=norm[:], in_=norm[:])
            nc.vector.tensor_tensor(
                out=by_run, in0=by_run, in1=norm[:].unsqueeze(2).to_broadcast([P, runs, width]), op=ALU.mult
            )

        gate_task = softmax_open(logits_task[:], gate_bias_task[:], TASK_GATES, "gate_task")
        gate_share = softmax_open(logits_share[:], gate_bias_share[:], SHARE_GATES, "gate_share")
        group_rows(0)
        softmax_close(gate_task, TASK_GATES, "gate_task")
        quantise_rows(0)
        softmax_close(gate_share, SHARE_GATES, "gate_share")

        pre_of = {}

        def issue_pass(q):
            r, c = divmod(q, PASSES)
            h, s = row_tile_of(r), source_of(r)
            if c == 0 and s == SHARED:
                pre_of[r] = work.tile([P, EXPERTS, UNITS], F32, name="pre_shared", bufs=2)
            if c == 0 and s != SHARED:
                pre_of[r] = work.tile([P, EXPERTS, UNITS], F32, name="pre_own", bufs=3)
            acc = psum_acc.tile([P, PASS_COLS], F32, name="acc")
            nc.tensor.matmul_mx(
                out=acc[:],
                lhsT=x_codes[:, h * P : (h + 1) * P].bitcast(FP8X4),
                lhsT_scale=x_scales[:, h * P : (h + 1) * P],
                rhs=words[:, s, 2 * c * PASS_COLS : 2 * (c + 1) * PASS_COLS].bitcast(FP4X4),
                rhs_scale=planes[:, s, c * PASS_COLS : (c + 1) * PASS_COLS],
                start=True,
                stop=True,
            )
            nc.vector.tensor_tensor(
                out=pre_of[r][:, :, c * PASS_UNITS : (c + 1) * PASS_UNITS].rearrange(
                    "p (g e) u -> p g u e", e=ROWS_IN_TURN
                ),
                in0=acc[:].rearrange("p (u g e) -> p g u e", u=PASS_UNITS, e=ROWS_IN_TURN),
                in1=bias_all[:, s, c * PASS_COLS : (c + 1) * PASS_COLS].rearrange(
                    "p (u g e) -> p g u e", u=PASS_UNITS, e=ROWS_IN_TURN
                ),
                op=ALU.add,
            )

        def gated(pre, e, gate_column, on_vector=False):
            term = work.tile([P, UNITS], F32, name="term", bufs=10)
            if on_vector:
                nc.vector.tensor_scalar(
                    out=term[:], in0=pre[:, e, :], scalar1=gate_column, scalar2=0.0, op0=ALU.mult, op1=ALU.max
                )
            else:
                nc.scalar.activation(out=term[:], in_=pre[:, e, :], func=ACT.Relu, scale=gate_column)
            return term

        terms_of = {}
        shared_part_of = {}

        def gate_step(n):
            r, e = divmod(n, EXPERTS)
            h, s = row_tile_of(r), source_of(r)
            j = s * EXPERTS + e
            if s == SHARED:
                terms_of[n] = [gated(pre_of[r], e, gate_share[:, h, j : j + 1])]
                if e % 2 == 0:
                    nc.vector.tensor_scalar_max(out=pre_of[r][:, e, :], in0=pre_of[r][:, e, :], scalar1=0.0)
                else:
                    nc.scalar.activation(out=pre_of[r][:, e, :], in_=pre_of[r][:, e, :], func=ACT.Relu)
            else:
                g = s * TASK_GATES + e
                terms_of[n] = [
                    gated(pre_of[r], e, gate_share[:, h, j : j + 1]),
                    gated(pre_of[r], e, gate_task[:, h, g : g + 1], n - GATE_LEAD + PASS_LEAD >= STEPS),
                ]
                shared_relu = pre_of[h * SOURCES][:, e, :]
                shared_gate = gate_task[:, h, g + EXPERTS : g + EXPERTS + 1]
                if e == 0:
                    shared_part_of[r] = work.tile([P, UNITS], F32, name="shared_part", bufs=3)
                    nc.vector.tensor_scalar_mul(out=shared_part_of[r][:], in0=shared_relu, scalar1=shared_gate)
                else:
                    nc.vector.scalar_tensor_tensor(
                        out=shared_part_of[r][:],
                        in0=shared_relu,
                        scalar=shared_gate,
                        in1=shared_part_of[r][:],
                        op0=ALU.mult,
                        op1=ALU.add,
                    )

        def add_block(total, term, k, first, last, as_transpose=True):
            nc.tensor.matmul(
                out=total[:, k, :],
                lhsT=term[:, k * P : (k + 1) * P],
                rhs=ident[:],
                is_transpose=as_transpose,
                start=(first and k == 0),
                stop=(last and k == UNIT_BLOCKS - 1),
            )

        totals = {}

        def sum_step(n):
            r, e = divmod(n, EXPERTS)
            s = source_of(r)
            if e == 0 and s == SHARED:
                totals["share"] = psum_sum.tile([P, UNIT_BLOCKS, P], F32, name="share_total", tag="total")
            if e == 0 and s != SHARED:
                totals["task"] = psum_sum.tile([P, UNIT_BLOCKS, P], F32, name="task_total", tag="total")
            terms = terms_of[n]
            for k in range(UNIT_BLOCKS):
                add_block(
                    totals["share"], terms[0], k, s == SHARED and e == 0, s == TASKS - 1 and e == EXPERTS - 1, k != 0
                )
                if s != SHARED:
                    add_block(totals["task"], terms[1], k, e == 0, e == EXPERTS - 1)

        def leave_psum(total, on_vector):
            turned_in = work.tile([P, UNIT_BLOCKS, P], F32, name="turned_in", bufs=3)
            if on_vector:
                nc.vector.tensor_copy(out=turned_in[:], in_=total[:])
            else:
                nc.scalar.copy(out=turned_in[:], in_=total[:])
            return turned_in

        def turn_and_store(turned_in, shared_part, rows):
            turned = psum_turn.tile([P, UNIT_BLOCKS, P], F32, name="turned", tag="turn")
            for k in range(UNIT_BLOCKS):
                nc.tensor.transpose(turned[:, k, :], turned_in[:, k, :], ident[:])
            result = work.tile([P, UNITS], F32, name="result", bufs=2)
            if shared_part is None:
                nc.scalar.copy(out=result[:], in_=turned[:].rearrange("p k u -> p (k u)"))
            else:
                nc.vector.tensor_tensor(
                    out=result[:], in0=turned[:].rearrange("p k u -> p (k u)"), in1=shared_part[:], op=ALU.add
                )
            nc.sync.dma_start(out=rows, in_=result[:])

        for q in range(PASSES):
            issue_pass(q)
        for n in range(GATE_LEAD):
            gate_step(n)
        for q in range(PASSES, PASS_LEAD):
            issue_pass(q)
        leaving = {}
        for n in range(STEPS + STORE_LAG):
            if n == 0:
                group_rows(1)
            if n == 1:
                quantise_rows(1)
            if n + GATE_LEAD < STEPS:
                gate_step(n + GATE_LEAD)
            if n + PASS_LEAD < STEPS:
                issue_pass(n + PASS_LEAD)
            if n < STEPS:
                sum_step(n)
                r, e = divmod(n, EXPERTS)
                h, s = row_tile_of(r), source_of(r)
                if e == EXPERTS - 1 and s != SHARED:
                    leaving[n + STORE_LAG] = [
                        (leave_psum(totals["task"], False), shared_part_of[r], out_0[s, h * P : (h + 1) * P, :])
                    ]
                if e == EXPERTS - 1 and s == TASKS - 1:
                    leaving[n + STORE_LAG].append((leave_psum(totals["share"], True), None, out_1[h * P : (h + 1) * P, :]))
            for turned_in, shared_part, rows in leaving.get(n, []):
                turn_and_store(turned_in, shared_part, rows)
